import numpy as np
import ml_dtypes


def mxq(x, axis, fmt="e4m3"):
    dtype, down = {"e4m3": (ml_dtypes.float8_e4m3fn, 7), "e5m2": (ml_dtypes.float8_e5m2, 14)}[fmt]
    v = np.moveaxis(np.asarray(x, np.float32).astype(ml_dtypes.bfloat16).astype(np.float64), axis, -1)
    blocks = v.reshape(v.shape[:-1] + (-1, 32))
    amax = np.abs(blocks).max(-1, keepdims=True)
    byte = np.maximum(np.where(amax > 0, np.frexp(amax)[1] - 1 + 127, 0) - down, 1)
    scale = np.exp2(byte - 127.0)
    codes = (blocks / scale).astype(np.float32).astype(dtype).astype(np.float64)
    return np.moveaxis((codes * scale).reshape(v.shape), -1, axis)


WIDE = False


def mx_kscale(k):
    if not WIDE:
        return np.ones(k)
    levels = np.array([10, -10, 5, -5, 0])
    if k % 512:
        return np.exp2(np.random.permutation(np.resize(levels, k // 32))).repeat(32)
    a = np.empty((k // 512, 16))
    for p in range(k // 512):
        a[p, :8] = np.random.permutation(np.resize(levels, 8))
        for g in range(8):
            far = levels[np.abs(levels - a[p, g]) >= 10]
            a[p, g + 8] = far[np.random.randint(len(far))]
    return np.exp2(a.ravel()).repeat(32)


BF16 = ml_dtypes.bfloat16


def bf(x):
    return np.asarray(x, np.float32).astype(BF16)


def f64(x):
    return np.asarray(x).astype(np.float64)


B, T, D, C, M = 2, 1024, 1024, 128, 4
NB = T // M
NEG = -1e30


def setup_inputs():
    s = mx_kscale(D)
    w = 1.0 / np.sqrt(D)
    return {
        "H": bf(np.random.standard_normal((B, T, D)) * s),
        "W_a_KV": bf(np.random.standard_normal((D, C)) * w / s[:, None]),
        "W_b_KV": bf(np.random.standard_normal((D, C)) * w / s[:, None]),
        "W_a_Z": bf(np.random.standard_normal((D, C)) * w / s[:, None]),
        "W_b_Z": bf(np.random.standard_normal((D, C)) * w / s[:, None]),
        "B_a": bf(np.random.standard_normal((M, C))),
        "B_b": bf(np.random.standard_normal((M, C))),
    }


def reference(H, W_a_KV, W_b_KV, W_a_Z, W_b_Z, B_a, B_b):
    Hq = mxq(f64(H), 2, "e4m3")
    C_a = (Hq @ mxq(f64(W_a_KV), 0, "e4m3")).reshape(B, NB, M, C)
    C_b = (Hq @ mxq(f64(W_b_KV), 0, "e4m3")).reshape(B, NB, M, C)
    Z_a = (Hq @ mxq(f64(W_a_Z), 0, "e4m3")).reshape(B, NB, M, C) + f64(B_a)
    Z_b = (Hq @ mxq(f64(W_b_Z), 0, "e4m3")).reshape(B, NB, M, C) + f64(B_b)
    Z_b_prev = np.concatenate([np.full((B, 1, M, C), NEG), Z_b[:, :-1]], axis=1)
    C_b_prev = np.concatenate([np.zeros((B, 1, M, C)), C_b[:, :-1]], axis=1)
    logits = np.concatenate([Z_a, Z_b_prev], axis=2)
    vals = np.concatenate([C_a, C_b_prev], axis=2)
    e = np.exp(logits - logits.max(axis=2, keepdims=True))
    probs = e / e.sum(axis=2, keepdims=True)
    return (probs * vals).sum(axis=2)

@@ -1,0 +1,303 @@
+from contextlib import ExitStack
+
+import concourse.mybir as mybir
+from concourse.masks import make_identity
+
+F32 = mybir.dt.float32
+BF16 = mybir.dt.bfloat16
+U32 = mybir.dt.uint32
+U8 = mybir.dt.uint8
+FP8X4 = mybir.dt.float8_e4m3fn_x4
+ACT = mybir.ActivationFunctionType
+ALU = mybir.AluOpType
+
+P = 128
+BATCH = 2
+TOKENS = 1024
+D = 1024
+CH = 128
+M = 4
+K_PASS = 512
+PASSES = D // K_PASS
+GROUP = 128
+GROUPS = BATCH * TOKENS // (M * GROUP)
+GROUPS_PER_BATCH = GROUPS // BATCH
+BLOCKS = TOKENS // M
+HALF = M // 2
+UNITS = 2 * GROUPS
+UNIT_COLS = HALF * GROUP
+NEG = -1e30
+ZA, ZB, CA, CB = 0, 1, 2, 3
+
+FLOPS = 2 * BATCH * TOKENS * D * 4 * CH
+
+
+def tile_tokencompressor_pa_kernel(tc, H, W_a_KV, W_b_KV, W_a_Z, W_b_Z, B_a, B_b, out):
+    nc = tc.nc
+    weights = [W_a_Z, W_b_Z, W_a_KV, W_b_KV]
+    h_groups = H.flatten_outer_dims().rearrange("(g i j) d -> g i j d", i=GROUP, j=M)
+    out_rows = out.flatten_outer_dims().rearrange("(g i) c -> i g c", i=GROUP)
+
+    with ExitStack() as stack:
+        keep = stack.enter_context(tc.tile_pool(name="keep", bufs=1))
+        work = stack.enter_context(tc.tile_pool(name="work", bufs=2))
+        psum = stack.enter_context(tc.psum_pool(name="psum", bufs=1))
+        stack.enter_context(tc.manual_schedule())
+
+        h_raw = [keep.tile([P, M, D], BF16, name="h_raw%d" % g) for g in range(GROUPS)]
+        w_raw = keep.tile([P, 4, PASSES, 4, CH], BF16)
+        bias_rows = keep.tile([P, P], BF16)
+
+        def load_h(u):
+            js = slice(HALF * (u % 2), HALF * (u % 2 + 1))
+            nc.sync.dma_start(out=h_raw[u // 2][:, js, :], in_=h_groups[u // 2][:, js, :])
+
+        def load_w(w):
+            nc.sync.dma_start(
+                out=w_raw[:, w],
+                in_=weights[w].rearrange("(c p t) n -> p c t n", c=PASSES, t=4),
+            )
+
+        nc.vector.memset(bias_rows[:], 0.0)
+        nc.sync.dma_start(out=bias_rows[0:M, :], in_=B_a)
+        nc.sync.dma_start(out=bias_rows[M : 2 * M, :], in_=B_b)
+        load_h(0)
+        load_w(ZA)
+        load_w(ZB)
+        load_h(1)
+        load_w(CB)
+        load_w(CA)
+        for u in range(2, UNITS):
+            load_h(u)
+
+        ident = keep.tile([P, P], F32)
+        make_identity(nc, ident[:])
+
+        z_all = [keep.tile([P, 2 * M, BLOCKS + 1], F32, name="z_all%d" % n) for n in range(BATCH)]
+        cb_all = [keep.tile([P, M, BLOCKS + 1], F32, name="cb_all%d" % n) for n in range(BATCH)]
+        for n in range(BATCH):
+            nc.vector.memset(z_all[n][:, M : 2 * M, 0:1], NEG)
+            nc.vector.memset(cb_all[n][:, :, 0:1], 0.0)
+        den_ps = psum.tile([P, GROUPS, CH], F32)
+        num_ps = psum.tile([P, GROUPS, CH], F32)
+
+        bias_rows32 = keep.tile([P, P], F32)
+        nc.vector.tensor_copy(out=bias_rows32[:], in_=bias_rows[:])
+        bias_ps = psum.tile([P, P], F32, tag="ca")
+        nc.tensor.transpose(out=bias_ps[:], in_=bias_rows32[:], identity=ident[:])
+        bias = keep.tile([P, 2 * M], F32)
+        nc.vector.tensor_copy(out=bias[:], in_=bias_ps[:, 0 : 2 * M])
+
+        w_grouped = keep.tile([P, 4, PASSES, CH, 4], BF16, align_bytes=64)
+        w_codes = keep.tile([P, 4, PASSES, CH], U32, align_bytes=64)
+        w_scales = keep.tile([P, 4, PASSES, CH], U8, align_bytes=64)
+
+        def regroup_w(w):
+            nc.vector.tensor_copy(out=w_grouped[:, w], in_=w_raw[:, w].rearrange("p c t n -> p c n t"))
+
+        def quantise_w(w):
+            nc.vector.quantize_mx(
+                out=w_codes[:, w].rearrange("p c n -> p (c n)").bitcast(FP8X4),
+                scales=w_scales[:, w].rearrange("p c n -> p (c n)"),
+                in_=w_grouped[:, w].rearrange("p c n t -> p (c n t)"),
+            )
+
+        xt, h_grouped, h_codes, h_scales = {}, {}, {}, {}
+        z_ps, cb_ps, ca_ps = {}, {}, {}
+        max4, max2, max1, terms = {}, {}, {}, {}
+
+        def transposes(u):
+            h_words = h_raw[u // 2].bitcast(F32)
+            for c in range(PASSES):
+                xt[u, c] = psum.tile([P, 2, HALF, GROUP], F32, name="xt", tag="xt", bufs=2)
+                for v in range(2):
+                    for jj in range(HALF):
+                        first = 256 * c + v
+                        nc.tensor.transpose(
+                            out=xt[u, c][:, v, jj, :],
+                            in_=h_words[:, HALF * (u % 2) + jj, first : 256 * (c + 1) : 2],
+                            identity=ident[:],
+                        )
+
+        def copies(u):
+            h_grouped[u] = work.tile([P, PASSES, UNIT_COLS, 4], BF16, align_bytes=64, name="h_grouped", tag="h_grouped")
+            h_grouped_words = h_grouped[u].bitcast(F32)
+            for c in range(PASSES):
+                nc.scalar.copy(out=h_grouped_words[:, c, :, :], in_=xt[u, c].rearrange("p v jj i -> p (jj i) v"))
+
+        def quantise_h(u):
+            h_codes[u] = work.tile([P, PASSES, UNIT_COLS], U32, align_bytes=64, name="h_codes", tag="h_codes", bufs=4)
+            h_scales[u] = work.tile([P, PASSES, UNIT_COLS], U8, align_bytes=64, name="h_scales", tag="h_scales", bufs=4)
+            nc.vector.quantize_mx(
+                out=h_codes[u].rearrange("p c col -> p (c col)").bitcast(FP8X4),
+                scales=h_scales[u].rearrange("p c col -> p (c col)"),
+                in_=h_grouped[u].rearrange("p c col t -> p (c col t)"),
+            )
+
+        def project(u, w, acc):
+            for c in range(PASSES):
+                nc.tensor.matmul_mx(
+                    out=acc.rearrange("p jj i -> p (jj i)"),
+                    lhsT=w_codes[:, w, c, :].bitcast(FP8X4),
+                    lhsT_scale=w_scales[:, w, c, :],
+                    rhs=h_codes[u][:, c, :].bitcast(FP8X4),
+                    rhs_scale=h_scales[u][:, c, :],
+                    start=(c == 0),
+                    stop=(c == PASSES - 1),
+                )
+
+        def project_z(u):
+            z_ps[u] = psum.tile([P, 2, HALF, GROUP], F32, name="z_ps", tag="z", bufs=2)
+            project(u, ZA, z_ps[u][:, 0])
+            project(u, ZB, z_ps[u][:, 1])
+
+        def project_cb(u):
+            cb_ps[u] = psum.tile([P, HALF, GROUP], F32, name="cb_ps", tag="cb")
+            project(u, CB, cb_ps[u])
+
+        def project_ca(u):
+            if u % 2 == 0:
+                ca_ps[u // 2] = psum.tile([P, M, GROUP], F32, name="ca_ps", tag="ca")
+            project(u, CA, ca_ps[u // 2][:, HALF * (u % 2) : HALF * (u % 2 + 1), :])
+
+        def place(g):
+            return g // GROUPS_PER_BATCH, GROUP * (g % GROUPS_PER_BATCH)
+
+        def add_bias(u):
+            n, first = place(u // 2)
+            for s in range(2):
+                for jj in range(HALF):
+                    k = M * s + HALF * (u % 2) + jj
+                    nc.scalar.activation(
+                        out=z_all[n][:, k, first + s : first + s + GROUP], in_=z_ps[u][:, s, jj, :],
+                        func=ACT.Identity, bias=bias[:, k : k + 1], scale=1.0,
+                    )
+
+        def copy_cb(u):
+            n, first = place(u // 2)
+            js = slice(HALF * (u % 2), HALF * (u % 2 + 1))
+            nc.scalar.copy(out=cb_all[n][:, js, first + 1 : first + 1 + GROUP], in_=cb_ps[u][:])
+
+        def logits(g):
+            n, first = place(g)
+            return z_all[n][:, :, first : first + GROUP]
+
+        def maximum(g):
+            max4[g] = work.tile([P, 4, GROUP], F32, name="max4", tag="max4")
+            nc.vector.tensor_tensor(out=max4[g][:], in0=logits(g)[:, 0:4, :], in1=logits(g)[:, 4:8, :], op=ALU.max)
+            max2[g] = work.tile([P, 2, GROUP], F32, name="max2", tag="max2")
+            nc.vector.tensor_tensor(out=max2[g][:], in0=max4[g][:, 0:2, :], in1=max4[g][:, 2:4, :], op=ALU.max)
+            max1[g] = work.tile([P, 1, GROUP], F32, name="max1", tag="max1")
+            nc.vector.tensor_tensor(out=max1[g][:], in0=max2[g][:, 0:1, :], in1=max2[g][:, 1:2, :], op=ALU.max)
+
+        def subtract_max(g, s):
+            if s == 0:
+                terms[g] = work.tile([P, 2, 2 * M, GROUP], F32, name="terms", tag="terms")
+            ks = slice(M * s, M * (s + 1))
+            nc.vector.tensor_tensor(
+                out=terms[g][:, 0, ks, :], in0=logits(g)[:, ks, :],
+                in1=max1[g].to_broadcast([P, M, GROUP]), op=ALU.subtract,
+            )
+
+        def exponentials(g, s):
+            ks = slice(M * s, M * (s + 1))
+            nc.scalar.activation(out=terms[g][:, 0, ks, :], in_=terms[g][:, 0, ks, :], func=ACT.Exp)
+
+        def times_values(g, s):
+            n, first = place(g)
+            ks = slice(M * s, M * (s + 1))
+            values = ca_ps[g][:] if s == 0 else cb_all[n][:, :, first : first + GROUP]
+            nc.vector.tensor_tensor(out=terms[g][:, 1, ks, :], in0=terms[g][:, 0, ks, :], in1=values, op=ALU.mult)
+
+        def sum_and_turn(g, q, total):
+            for k in range(2 * M):
+                nc.tensor.matmul(
+                    out=total[:, g, :], lhsT=terms[g][:, q, k, :], rhs=ident[:], is_transpose=True,
+                    start=(k == 0), stop=(k == 2 * M - 1),
+                )
+
+        rsqrt = keep.tile([P, GROUPS, CH], F32)
+        recip = keep.tile([P, GROUPS, CH], F32)
+        result_rows = keep.tile([P, GROUPS, CH], F32)
+
+        def reciprocal_of_sum(g0, g1):
+            nc.scalar.activation(out=rsqrt[:, g0:g1, :], in_=den_ps[:, g0:g1, :], func=ACT.Abs_reciprocal_sqrt)
+            nc.scalar.activation(out=recip[:, g0:g1, :], in_=rsqrt[:, g0:g1, :], func=ACT.Square)
+
+        def finish(g0, g1):
+            nc.vector.tensor_tensor(
+                out=result_rows[:, g0:g1, :], in0=num_ps[:, g0:g1, :], in1=recip[:, g0:g1, :], op=ALU.mult
+            )
+            nc.sync.dma_start(out=out_rows[:, g0:g1, :], in_=result_rows[:, g0:g1, :])
+
+        transposes(0)
+        copies(0)
+        transposes(1)
+        regroup_w(ZA)
+        regroup_w(ZB)
+        quantise_w(ZA)
+        quantise_w(ZB)
+        quantise_h(0)
+        regroup_w(CB)
+        quantise_w(CB)
+        project_z(0)
+        project_cb(0)
+        copies(1)
+        transposes(2)
+        quantise_h(1)
+        regroup_w(CA)
+        quantise_w(CA)
+        add_bias(0)
+        copy_cb(0)
+        project_z(1)
+        project_cb(1)
+        project_ca(0)
+        project_ca(1)
+        copies(2)
+
+        for g in range(GROUPS):
+            u = 2 * g + 1
+            add_bias(u)
+            copy_cb(u)
+            if u + 2 < UNITS:
+                transposes(u + 2)
+            if g > 0:
+                sum_and_turn(g - 1, 0, den_ps)
+            if u + 1 < UNITS:
+                quantise_h(u + 1)
+                project_z(u + 1)
+                project_cb(u + 1)
+            maximum(g)
+            subtract_max(g, 0)
+            if u + 2 < UNITS:
+                copies(u + 2)
+            if u + 3 < UNITS:
+                transposes(u + 3)
+            if g > 0:
+                sum_and_turn(g - 1, 1, num_ps)
+            if u + 2 < UNITS:
+                quantise_h(u + 2)
+            subtract_max(g, 1)
+            if u + 1 < UNITS:
+                add_bias(u + 1)
+                copy_cb(u + 1)
+            if u + 2 < UNITS:
+                project_z(u + 2)
+                project_cb(u + 2)
+            exponentials(g, 0)
+            exponentials(g, 1)
+            times_values(g, 0)
+            if u + 2 < UNITS:
+                project_ca(u + 1)
+                project_ca(u + 2)
+            times_values(g, 1)
+            if u + 3 < UNITS:
+                copies(u + 3)
+
+        last = GROUPS - 1
+        sum_and_turn(last, 0, den_ps)
+        sum_and_turn(last, 1, num_ps)
+        reciprocal_of_sum(0, last)
+        reciprocal_of_sum(last, GROUPS)
+        finish(0, last)
+        finish(last, GROUPS)

@@ -59,34 +59,33 @@ def tile_tokencompressor_pa_kernel(tc, H, W_a_KV, W_b_KV, W_a_Z, W_b_Z, B_a, B_b
             )
 
         nc.vector.memset(bias_rows[:], 0.0)
+        load_h(0)
         nc.sync.dma_start(out=bias_rows[0:M, :], in_=B_a)
         nc.sync.dma_start(out=bias_rows[M : 2 * M, :], in_=B_b)
-        load_h(0)
         load_w(ZA)
-        load_w(ZB)
         load_h(1)
-        load_w(CB)
+        load_w(ZB)
+        load_h(2)
         load_w(CA)
-        for u in range(2, UNITS):
+        load_w(CB)
+        for u in range(3, UNITS):
             load_h(u)
 
         ident = keep.tile([P, P], F32)
         make_identity(nc, ident[:])
 
         z_all = [keep.tile([P, 2 * M, BLOCKS + 1], F32, name="z_all%d" % n) for n in range(BATCH)]
-        cb_all = [keep.tile([P, M, BLOCKS + 1], F32, name="cb_all%d" % n) for n in range(BATCH)]
         for n in range(BATCH):
             nc.vector.memset(z_all[n][:, M : 2 * M, 0:1], NEG)
-            nc.vector.memset(cb_all[n][:, :, 0:1], 0.0)
+        cb_edge = keep.tile([P, GROUPS, M, 1], F32)
+        nc.vector.memset(cb_edge[:], 0.0)
         den_ps = psum.tile([P, GROUPS, CH], F32)
         num_ps = psum.tile([P, GROUPS, CH], F32)
 
         bias_rows32 = keep.tile([P, P], F32)
-        nc.vector.tensor_copy(out=bias_rows32[:], in_=bias_rows[:])
-        bias_ps = psum.tile([P, P], F32, tag="ca")
-        nc.tensor.transpose(out=bias_ps[:], in_=bias_rows32[:], identity=ident[:])
         bias = keep.tile([P, 2 * M], F32)
-        nc.vector.tensor_copy(out=bias[:], in_=bias_ps[:, 0 : 2 * M])
+
+        bias_ps = psum.tile([P, P], F32, tag="ca")
 
         w_grouped = keep.tile([P, 4, PASSES, CH, 4], BF16, align_bytes=64)
         w_codes = keep.tile([P, 4, PASSES, CH], U32, align_bytes=64)
@@ -95,11 +94,11 @@ def tile_tokencompressor_pa_kernel(tc, H, W_a_KV, W_b_KV, W_a_Z, W_b_Z, B_a, B_b
         def regroup_w(w):
             nc.vector.tensor_copy(out=w_grouped[:, w], in_=w_raw[:, w].rearrange("p c t n -> p c n t"))
 
-        def quantise_w(w):
+        def quantise_w(w0, w1):
             nc.vector.quantize_mx(
-                out=w_codes[:, w].rearrange("p c n -> p (c n)").bitcast(FP8X4),
-                scales=w_scales[:, w].rearrange("p c n -> p (c n)"),
-                in_=w_grouped[:, w].rearrange("p c n t -> p (c n t)"),
+                out=w_codes[:, w0:w1].rearrange("p w c n -> p (w c n)").bitcast(FP8X4),
+                scales=w_scales[:, w0:w1].rearrange("p w c n -> p (w c n)"),
+                in_=w_grouped[:, w0:w1].rearrange("p w c n t -> p (w c n t)"),
             )
 
         xt, h_grouped, h_codes, h_scales = {}, {}, {}, {}
@@ -120,14 +119,14 @@ def tile_tokencompressor_pa_kernel(tc, H, W_a_KV, W_b_KV, W_a_Z, W_b_Z, B_a, B_b
                         )
 
         def copies(u):
-            h_grouped[u] = work.tile([P, PASSES, UNIT_COLS, 4], BF16, align_bytes=64, name="h_grouped", tag="h_grouped")
+            h_grouped[u] = work.tile([P, PASSES, UNIT_COLS, 4], BF16, align_bytes=64, name="h_grouped", tag="h_grouped", bufs=4)
             h_grouped_words = h_grouped[u].bitcast(F32)
             for c in range(PASSES):
                 nc.scalar.copy(out=h_grouped_words[:, c, :, :], in_=xt[u, c].rearrange("p v jj i -> p (jj i) v"))
 
         def quantise_h(u):
-            h_codes[u] = work.tile([P, PASSES, UNIT_COLS], U32, align_bytes=64, name="h_codes", tag="h_codes", bufs=4)
-            h_scales[u] = work.tile([P, PASSES, UNIT_COLS], U8, align_bytes=64, name="h_scales", tag="h_scales", bufs=4)
+            h_codes[u] = work.tile([P, PASSES, UNIT_COLS], U32, align_bytes=64, name="h_codes", tag="h_codes", bufs=6)
+            h_scales[u] = work.tile([P, PASSES, UNIT_COLS], U8, align_bytes=64, name="h_scales", tag="h_scales", bufs=6)
             nc.vector.quantize_mx(
                 out=h_codes[u].rearrange("p c col -> p (c col)").bitcast(FP8X4),
                 scales=h_scales[u].rearrange("p c col -> p (c col)"),
@@ -151,14 +150,15 @@ def tile_tokencompressor_pa_kernel(tc, H, W_a_KV, W_b_KV, W_a_Z, W_b_Z, B_a, B_b
             project(u, ZA, z_ps[u][:, 0])
             project(u, ZB, z_ps[u][:, 1])
 
-        def project_cb(u):
-            cb_ps[u] = psum.tile([P, HALF, GROUP], F32, name="cb_ps", tag="cb")
-            project(u, CB, cb_ps[u])
+        def project_ca(g):
+            ca_ps[g] = psum.tile([P, M, GROUP], F32, name="ca_ps", tag="ca")
+            for half in range(2):
+                project(2 * g + half, CA, ca_ps[g][:, HALF * half : HALF * (half + 1), :])
 
-        def project_ca(u):
-            if u % 2 == 0:
-                ca_ps[u // 2] = psum.tile([P, M, GROUP], F32, name="ca_ps", tag="ca")
-            project(u, CA, ca_ps[u // 2][:, HALF * (u % 2) : HALF * (u % 2 + 1), :])
+        def project_cb(g):
+            cb_ps[g] = psum.tile([P, M, GROUP], F32, name="cb_ps", tag="cb")
+            for half in range(2):
+                project(2 * g + half, CB, cb_ps[g][:, HALF * half : HALF * (half + 1), :])
 
         def place(g):
             return g // GROUPS_PER_BATCH, GROUP * (g % GROUPS_PER_BATCH)
@@ -173,26 +173,33 @@ def tile_tokencompressor_pa_kernel(tc, H, W_a_KV, W_b_KV, W_a_Z, W_b_Z, B_a, B_b
                         func=ACT.Identity, bias=bias[:, k : k + 1], scale=1.0,
                     )
 
-        def copy_cb(u):
-            n, first = place(u // 2)
-            js = slice(HALF * (u % 2), HALF * (u % 2 + 1))
-            nc.scalar.copy(out=cb_all[n][:, js, first + 1 : first + 1 + GROUP], in_=cb_ps[u][:])
+        def copy_cb_edge(g):
+            nc.scalar.copy(out=cb_edge[:, g + 1], in_=cb_ps[g][:, :, GROUP - 1 : GROUP])
 
         def logits(g):
             n, first = place(g)
             return z_all[n][:, :, first : first + GROUP]
 
-        def maximum(g):
-            max4[g] = work.tile([P, 4, GROUP], F32, name="max4", tag="max4")
-            nc.vector.tensor_tensor(out=max4[g][:], in0=logits(g)[:, 0:4, :], in1=logits(g)[:, 4:8, :], op=ALU.max)
+        def maximum_of_unit(u):
+            g, half = u // 2, u % 2
+            if half == 0:
+                max4[g] = work.tile([P, M, GROUP], F32, name="max4", tag="max4")
+            js = slice(HALF * half, HALF * (half + 1))
+            nc.vector.tensor_tensor(
+                out=max4[g][:, js, :], in0=logits(g)[:, 0:M, :][:, js, :], in1=logits(g)[:, M : 2 * M, :][:, js, :], op=ALU.max
+            )
+
+        def maximum_2(g):
             max2[g] = work.tile([P, 2, GROUP], F32, name="max2", tag="max2")
             nc.vector.tensor_tensor(out=max2[g][:], in0=max4[g][:, 0:2, :], in1=max4[g][:, 2:4, :], op=ALU.max)
+
+        def maximum_1(g):
             max1[g] = work.tile([P, 1, GROUP], F32, name="max1", tag="max1")
             nc.vector.tensor_tensor(out=max1[g][:], in0=max2[g][:, 0:1, :], in1=max2[g][:, 1:2, :], op=ALU.max)
 
         def subtract_max(g, s):
             if s == 0:
-                terms[g] = work.tile([P, 2, 2 * M, GROUP], F32, name="terms", tag="terms")
+                terms[g] = work.tile([P, 2, 2 * M, GROUP], F32, name="terms", tag="terms", bufs=3)
             ks = slice(M * s, M * (s + 1))
             nc.vector.tensor_tensor(
                 out=terms[g][:, 0, ks, :], in0=logits(g)[:, ks, :],
@@ -204,10 +211,16 @@ def tile_tokencompressor_pa_kernel(tc, H, W_a_KV, W_b_KV, W_a_Z, W_b_Z, B_a, B_b
             nc.scalar.activation(out=terms[g][:, 0, ks, :], in_=terms[g][:, 0, ks, :], func=ACT.Exp)
 
         def times_values(g, s):
-            n, first = place(g)
             ks = slice(M * s, M * (s + 1))
-            values = ca_ps[g][:] if s == 0 else cb_all[n][:, :, first : first + GROUP]
-            nc.vector.tensor_tensor(out=terms[g][:, 1, ks, :], in0=terms[g][:, 0, ks, :], in1=values, op=ALU.mult)
+            shift = s
+            nc.vector.tensor_tensor(
+                out=terms[g][:, 1, ks, shift:], in0=terms[g][:, 0, ks, shift:],
+                in1=(ca_ps, cb_ps)[s][g][:, :, 0 : GROUP - shift], op=ALU.mult,
+            )
+            if s == 1:
+                nc.vector.tensor_tensor(
+                    out=terms[g][:, 1, ks, 0:1], in0=terms[g][:, 0, ks, 0:1], in1=cb_edge[:, g], op=ALU.mult
+                )
 
         def sum_and_turn(g, q, total):
             for k in range(2 * M):
@@ -232,69 +245,79 @@ def tile_tokencompressor_pa_kernel(tc, H, W_a_KV, W_b_KV, W_a_Z, W_b_Z, B_a, B_b
 
         transposes(0)
         copies(0)
-        transposes(1)
+        nc.vector.tensor_copy(out=bias_rows32[:], in_=bias_rows[:])
+        nc.tensor.transpose(out=bias_ps[:], in_=bias_rows32[:], identity=ident[:])
         regroup_w(ZA)
-        regroup_w(ZB)
-        quantise_w(ZA)
-        quantise_w(ZB)
+        quantise_w(ZA, ZA + 1)
+        nc.vector.tensor_copy(out=bias[:], in_=bias_ps[:, 0 : 2 * M])
+        transposes(1)
         quantise_h(0)
-        regroup_w(CB)
-        quantise_w(CB)
-        project_z(0)
-        project_cb(0)
         copies(1)
-        transposes(2)
+        regroup_w(ZB)
+        quantise_w(ZB, ZB + 1)
         quantise_h(1)
-        regroup_w(CA)
-        quantise_w(CA)
-        add_bias(0)
-        copy_cb(0)
-        project_z(1)
-        project_cb(1)
-        project_ca(0)
-        project_ca(1)
+        transposes(2)
         copies(2)
-
-        for g in range(GROUPS):
-            u = 2 * g + 1
-            add_bias(u)
-            copy_cb(u)
-            if u + 2 < UNITS:
-                transposes(u + 2)
-            if g > 0:
-                sum_and_turn(g - 1, 0, den_ps)
-            if u + 1 < UNITS:
-                quantise_h(u + 1)
-                project_z(u + 1)
-                project_cb(u + 1)
-            maximum(g)
-            subtract_max(g, 0)
-            if u + 2 < UNITS:
-                copies(u + 2)
-            if u + 3 < UNITS:
-                transposes(u + 3)
-            if g > 0:
-                sum_and_turn(g - 1, 1, num_ps)
-            if u + 2 < UNITS:
-                quantise_h(u + 2)
-            subtract_max(g, 1)
-            if u + 1 < UNITS:
-                add_bias(u + 1)
-                copy_cb(u + 1)
-            if u + 2 < UNITS:
-                project_z(u + 2)
-                project_cb(u + 2)
-            exponentials(g, 0)
-            exponentials(g, 1)
-            times_values(g, 0)
-            if u + 2 < UNITS:
-                project_ca(u + 1)
-                project_ca(u + 2)
-            times_values(g, 1)
-            if u + 3 < UNITS:
-                copies(u + 3)
+        project_z(0)
+        project_z(1)
+        transposes(3)
+        add_bias(0)
+        regroup_w(CA)
+        regroup_w(CB)
+        maximum_of_unit(0)
+        add_bias(1)
+        quantise_w(CA, CB + 1)
 
         last = GROUPS - 1
+        for g in range(last):
+            u = 2 * g
+            copies(u + 3)
+            if g > 0:
+                times_values(g - 1, 0)
+            maximum_of_unit(u + 1)
+            if g > 0:
+                times_values(g - 1, 1)
+                sum_and_turn(g - 1, 0, den_ps)
+            if u + 4 < UNITS:
+                transposes(u + 4)
+                copies(u + 4)
+            maximum_2(g)
+            quantise_h(u + 2)
+            project_z(u + 2)
+            maximum_1(g)
+            quantise_h(u + 3)
+            project_z(u + 3)
+            add_bias(u + 2)
+            subtract_max(g, 0)
+            exponentials(g, 0)
+            subtract_max(g, 1)
+            project_ca(g)
+            project_cb(g)
+            add_bias(u + 3)
+            exponentials(g, 1)
+            if (g + 1) % GROUPS_PER_BATCH > 0:
+                copy_cb_edge(g)
+            maximum_of_unit(u + 2)
+            if u + 5 < UNITS:
+                transposes(u + 5)
+            if g > 0:
+                sum_and_turn(g - 1, 1, num_ps)
+
+        times_values(last - 1, 0)
+        maximum_of_unit(UNITS - 1)
+        times_values(last - 1, 1)
+        maximum_2(last)
+        project_ca(last)
+        project_cb(last)
+        maximum_1(last)
+        sum_and_turn(last - 1, 0, den_ps)
+        sum_and_turn(last - 1, 1, num_ps)
+        subtract_max(last, 0)
+        exponentials(last, 0)
+        subtract_max(last, 1)
+        exponentials(last, 1)
+        times_values(last, 0)
+        times_values(last, 1)
         sum_and_turn(last, 0, den_ps)
         sum_and_turn(last, 1, num_ps)
         reciprocal_of_sum(0, last)

@@ -29,6 +29,8 @@ UNIT_COLS = HALF * GROUP
 NEG = -1e30
 ZA, ZB, CA, CB = 0, 1, 2, 3
 
+BANKS = 6
+
 FLOPS = 2 * BATCH * TOKENS * D * 4 * CH
 
 
@@ -85,7 +87,7 @@ def tile_tokencompressor_pa_kernel(tc, H, W_a_KV, W_b_KV, W_a_Z, W_b_Z, B_a, B_b
         bias_rows32 = keep.tile([P, P], F32)
         bias = keep.tile([P, 2 * M], F32)
 
-        bias_ps = psum.tile([P, P], F32, tag="ca")
+        bias_ps = psum.tile([P, P], F32, tag="bank", bufs=BANKS)
 
         w_grouped = keep.tile([P, 4, PASSES, CH, 4], BF16, align_bytes=64)
         w_codes = keep.tile([P, 4, PASSES, CH], U32, align_bytes=64)
@@ -108,7 +110,7 @@ def tile_tokencompressor_pa_kernel(tc, H, W_a_KV, W_b_KV, W_a_Z, W_b_Z, B_a, B_b
         def transposes(u):
             h_words = h_raw[u // 2].bitcast(F32)
             for c in range(PASSES):
-                xt[u, c] = psum.tile([P, 2, HALF, GROUP], F32, name="xt", tag="xt", bufs=2)
+                xt[u, c] = psum.tile([P, 2, HALF, GROUP], F32, name="xt", tag="bank", bufs=BANKS)
                 for v in range(2):
                     for jj in range(HALF):
                         first = 256 * c + v
@@ -118,15 +120,16 @@ def tile_tokencompressor_pa_kernel(tc, H, W_a_KV, W_b_KV, W_a_Z, W_b_Z, B_a, B_b
                             identity=ident[:],
                         )
 
-        def copies(u):
+        def copies(u, vector_passes=()):
             h_grouped[u] = work.tile([P, PASSES, UNIT_COLS, 4], BF16, align_bytes=64, name="h_grouped", tag="h_grouped", bufs=4)
             h_grouped_words = h_grouped[u].bitcast(F32)
             for c in range(PASSES):
-                nc.scalar.copy(out=h_grouped_words[:, c, :, :], in_=xt[u, c].rearrange("p v jj i -> p (jj i) v"))
+                copy = nc.vector.tensor_copy if c in vector_passes else nc.scalar.copy
+                copy(out=h_grouped_words[:, c, :, :], in_=xt[u, c].rearrange("p v jj i -> p (jj i) v"))
 
         def quantise_h(u):
-            h_codes[u] = work.tile([P, PASSES, UNIT_COLS], U32, align_bytes=64, name="h_codes", tag="h_codes", bufs=6)
-            h_scales[u] = work.tile([P, PASSES, UNIT_COLS], U8, align_bytes=64, name="h_scales", tag="h_scales", bufs=6)
+            h_codes[u] = work.tile([P, PASSES, UNIT_COLS], U32, align_bytes=64, name="h_codes", tag="h_codes", bufs=UNITS)
+            h_scales[u] = work.tile([P, PASSES, UNIT_COLS], U8, align_bytes=64, name="h_scales", tag="h_scales", bufs=UNITS)
             nc.vector.quantize_mx(
                 out=h_codes[u].rearrange("p c col -> p (c col)").bitcast(FP8X4),
                 scales=h_scales[u].rearrange("p c col -> p (c col)"),
@@ -146,19 +149,18 @@ def tile_tokencompressor_pa_kernel(tc, H, W_a_KV, W_b_KV, W_a_Z, W_b_Z, B_a, B_b
                 )
 
         def project_z(u):
-            z_ps[u] = psum.tile([P, 2, HALF, GROUP], F32, name="z_ps", tag="z", bufs=2)
+            z_ps[u] = psum.tile([P, 2, HALF, GROUP], F32, name="z_ps", tag="bank", bufs=BANKS)
             project(u, ZA, z_ps[u][:, 0])
             project(u, ZB, z_ps[u][:, 1])
 
-        def project_ca(g):
-            ca_ps[g] = psum.tile([P, M, GROUP], F32, name="ca_ps", tag="ca")
-            for half in range(2):
-                project(2 * g + half, CA, ca_ps[g][:, HALF * half : HALF * (half + 1), :])
-
-        def project_cb(g):
-            cb_ps[g] = psum.tile([P, M, GROUP], F32, name="cb_ps", tag="cb")
-            for half in range(2):
-                project(2 * g + half, CB, cb_ps[g][:, HALF * half : HALF * (half + 1), :])
+        def project_c(u):
+            g, half = u // 2, u % 2
+            if half == 0:
+                ca_ps[g] = psum.tile([P, M, GROUP], F32, name="ca_ps", tag="bank", bufs=BANKS)
+                cb_ps[g] = psum.tile([P, M, GROUP], F32, name="cb_ps", tag="bank", bufs=BANKS)
+            js = slice(HALF * half, HALF * (half + 1))
+            project(u, CA, ca_ps[g][:, js, :])
+            project(u, CB, cb_ps[g][:, js, :])
 
         def place(g):
             return g // GROUPS_PER_BATCH, GROUP * (g % GROUPS_PER_BATCH)
@@ -222,19 +224,34 @@ def tile_tokencompressor_pa_kernel(tc, H, W_a_KV, W_b_KV, W_a_Z, W_b_Z, B_a, B_b
                     out=terms[g][:, 1, ks, 0:1], in0=terms[g][:, 0, ks, 0:1], in1=cb_edge[:, g], op=ALU.mult
                 )
 
-        def sum_and_turn(g, q, total):
-            for k in range(2 * M):
+        pairs = {}
+
+        def add_pairs(g, q):
+            if q == 0:
+                pairs[g] = work.tile([P, 2, M, GROUP], F32, name="pairs", tag="pairs")
+            nc.vector.tensor_tensor(
+                out=pairs[g][:, q], in0=terms[g][:, q, 0:M, :], in1=terms[g][:, q, M : 2 * M, :], op=ALU.add
+            )
+
+        def sum_and_turn(total, g, parts):
+            for i, part in enumerate(parts):
                 nc.tensor.matmul(
-                    out=total[:, g, :], lhsT=terms[g][:, q, k, :], rhs=ident[:], is_transpose=True,
-                    start=(k == 0), stop=(k == 2 * M - 1),
+                    out=total[:, g, :], lhsT=part, rhs=ident[:], is_transpose=True,
+                    start=(i == 0), stop=(i == len(parts) - 1),
                 )
+
+        def sum_pairs(g):
+            sum_and_turn(den_ps, g, [pairs[g][:, 0, j, :] for j in range(M)])
+            sum_and_turn(num_ps, g, [pairs[g][:, 1, j, :] for j in range(M)])
 
         rsqrt = keep.tile([P, GROUPS, CH], F32)
         recip = keep.tile([P, GROUPS, CH], F32)
         result_rows = keep.tile([P, GROUPS, CH], F32)
 
-        def reciprocal_of_sum(g0, g1):
+        def rsqrt_of_sum(g0, g1):
             nc.scalar.activation(out=rsqrt[:, g0:g1, :], in_=den_ps[:, g0:g1, :], func=ACT.Abs_reciprocal_sqrt)
+
+        def reciprocal_of_sum(g0, g1):
             nc.scalar.activation(out=recip[:, g0:g1, :], in_=rsqrt[:, g0:g1, :], func=ACT.Square)
 
         def finish(g0, g1):
@@ -244,9 +261,9 @@ def tile_tokencompressor_pa_kernel(tc, H, W_a_KV, W_b_KV, W_a_Z, W_b_Z, B_a, B_b
             nc.sync.dma_start(out=out_rows[:, g0:g1, :], in_=result_rows[:, g0:g1, :])
 
         transposes(0)
-        copies(0)
         nc.vector.tensor_copy(out=bias_rows32[:], in_=bias_rows[:])
         nc.tensor.transpose(out=bias_ps[:], in_=bias_rows32[:], identity=ident[:])
+        copies(0)
         regroup_w(ZA)
         quantise_w(ZA, ZA + 1)
         nc.vector.tensor_copy(out=bias[:], in_=bias_ps[:, 0 : 2 * M])
@@ -259,68 +276,94 @@ def tile_tokencompressor_pa_kernel(tc, H, W_a_KV, W_b_KV, W_a_Z, W_b_Z, B_a, B_b
         transposes(2)
         copies(2)
         project_z(0)
+        regroup_w(CA)
         project_z(1)
         transposes(3)
         add_bias(0)
-        regroup_w(CA)
+        quantise_h(2)
         regroup_w(CB)
         maximum_of_unit(0)
         add_bias(1)
         quantise_w(CA, CB + 1)
+        maximum_of_unit(1)
+        copies(3)
+        transposes(4)
+        maximum_2(0)
+        quantise_h(3)
+        maximum_1(0)
+        copies(4)
+        transposes(5)
+        subtract_max(0, 0)
+        subtract_max(0, 1)
+        quantise_h(4)
+        copies(5)
+        exponentials(0, 0)
+        exponentials(0, 1)
+        transposes(6)
+        quantise_h(5)
+        transposes(7)
+        copies(6, (1,))
+        copies(7, (1,))
+        project_z(2)
+        project_z(3)
+        quantise_h(6)
+        project_c(0)
+        project_c(1)
+        quantise_h(7)
+        add_bias(2)
+        add_bias(3)
+        project_z(4)
+        project_z(5)
+        copy_cb_edge(0)
 
         last = GROUPS - 1
-        for g in range(last):
+        for g in range(1, last):
             u = 2 * g
-            copies(u + 3)
-            if g > 0:
-                times_values(g - 1, 0)
+            maximum_of_unit(u)
             maximum_of_unit(u + 1)
-            if g > 0:
-                times_values(g - 1, 1)
-                sum_and_turn(g - 1, 0, den_ps)
-            if u + 4 < UNITS:
-                transposes(u + 4)
-                copies(u + 4)
+            times_values(g - 1, 0)
             maximum_2(g)
-            quantise_h(u + 2)
-            project_z(u + 2)
+            times_values(g - 1, 1)
             maximum_1(g)
-            quantise_h(u + 3)
-            project_z(u + 3)
-            add_bias(u + 2)
+            if u + 2 < UNITS:
+                add_bias(u + 2)
+                add_bias(u + 3)
+            project_c(u)
+            project_c(u + 1)
+            if u + 4 < UNITS:
+                project_z(u + 4)
+                project_z(u + 5)
             subtract_max(g, 0)
             exponentials(g, 0)
             subtract_max(g, 1)
-            project_ca(g)
-            project_cb(g)
-            add_bias(u + 3)
             exponentials(g, 1)
             if (g + 1) % GROUPS_PER_BATCH > 0:
                 copy_cb_edge(g)
-            maximum_of_unit(u + 2)
-            if u + 5 < UNITS:
-                transposes(u + 5)
-            if g > 0:
-                sum_and_turn(g - 1, 1, num_ps)
+            sum_and_turn(den_ps, g - 1, [terms[g - 1][:, 0, k, :] for k in range(2 * M)])
+            sum_and_turn(num_ps, g - 1, [terms[g - 1][:, 1, k, :] for k in range(2 * M)])
 
-        times_values(last - 1, 0)
-        maximum_of_unit(UNITS - 1)
-        times_values(last - 1, 1)
+        u = 2 * last
+        maximum_of_unit(u)
+        maximum_of_unit(u + 1)
         maximum_2(last)
-        project_ca(last)
-        project_cb(last)
         maximum_1(last)
-        sum_and_turn(last - 1, 0, den_ps)
-        sum_and_turn(last - 1, 1, num_ps)
+        project_c(u)
+        project_c(u + 1)
+        sum_and_turn(den_ps, last - 1, [terms[last - 1][:, 0, k, :] for k in range(2 * M)])
         subtract_max(last, 0)
         exponentials(last, 0)
         subtract_max(last, 1)
         exponentials(last, 1)
+        times_values(last - 1, 0)
+        times_values(last - 1, 1)
         times_values(last, 0)
         times_values(last, 1)
-        sum_and_turn(last, 0, den_ps)
-        sum_and_turn(last, 1, num_ps)
-        reciprocal_of_sum(0, last)
-        reciprocal_of_sum(last, GROUPS)
-        finish(0, last)
-        finish(last, GROUPS)
+        sum_and_turn(den_ps, last, [terms[last][:, 0, k, :] for k in range(2 * M)])
+        sum_and_turn(num_ps, last - 1, [terms[last - 1][:, 1, k, :] for k in range(2 * M)])
+        sum_and_turn(num_ps, last, [terms[last][:, 1, k, :] for k in range(2 * M)])
+        rsqrt_of_sum(0, last - 1)
+        rsqrt_of_sum(last - 1, GROUPS)
+        reciprocal_of_sum(0, last - 1)
+        reciprocal_of_sum(last - 1, GROUPS)
+        finish(0, last - 1)
+        finish(last - 1, GROUPS)

@@ -199,60 +199,49 @@ def tile_tokencompressor_pa_kernel(tc, H, W_a_KV, W_b_KV, W_a_Z, W_b_Z, B_a, B_b
             max1[g] = work.tile([P, 1, GROUP], F32, name="max1", tag="max1")
             nc.vector.tensor_tensor(out=max1[g][:], in0=max2[g][:, 0:1, :], in1=max2[g][:, 1:2, :], op=ALU.max)
 
-        def subtract_max(g, s):
-            if s == 0:
+        def subtract_max(g, s, j0=0, j1=M):
+            if s == 0 and j0 == 0:
                 terms[g] = work.tile([P, 2, 2 * M, GROUP], F32, name="terms", tag="terms", bufs=3)
-            ks = slice(M * s, M * (s + 1))
+            ks = slice(M * s + j0, M * s + j1)
             nc.vector.tensor_tensor(
                 out=terms[g][:, 0, ks, :], in0=logits(g)[:, ks, :],
-                in1=max1[g].to_broadcast([P, M, GROUP]), op=ALU.subtract,
+                in1=max1[g].to_broadcast([P, j1 - j0, GROUP]), op=ALU.subtract,
             )
 
-        def exponentials(g, s):
-            ks = slice(M * s, M * (s + 1))
+        def exponentials(g, s, j0=0, j1=M):
+            ks = slice(M * s + j0, M * s + j1)
             nc.scalar.activation(out=terms[g][:, 0, ks, :], in_=terms[g][:, 0, ks, :], func=ACT.Exp)
 
-        def times_values(g, s):
-            ks = slice(M * s, M * (s + 1))
+        def times_values(g, s, j0=0, j1=M):
+            ks = slice(M * s + j0, M * s + j1)
             shift = s
             nc.vector.tensor_tensor(
                 out=terms[g][:, 1, ks, shift:], in0=terms[g][:, 0, ks, shift:],
-                in1=(ca_ps, cb_ps)[s][g][:, :, 0 : GROUP - shift], op=ALU.mult,
+                in1=(ca_ps, cb_ps)[s][g][:, j0:j1, 0 : GROUP - shift], op=ALU.mult,
             )
-            if s == 1:
-                nc.vector.tensor_tensor(
-                    out=terms[g][:, 1, ks, 0:1], in0=terms[g][:, 0, ks, 0:1], in1=cb_edge[:, g], op=ALU.mult
-                )
 
-        pairs = {}
-
-        def add_pairs(g, q):
-            if q == 0:
-                pairs[g] = work.tile([P, 2, M, GROUP], F32, name="pairs", tag="pairs")
+        def times_edge_values(g):
+            ks = slice(M, 2 * M)
             nc.vector.tensor_tensor(
-                out=pairs[g][:, q], in0=terms[g][:, q, 0:M, :], in1=terms[g][:, q, M : 2 * M, :], op=ALU.add
+                out=terms[g][:, 1, ks, 0:1], in0=terms[g][:, 0, ks, 0:1], in1=cb_edge[:, g], op=ALU.mult
             )
 
-        def sum_and_turn(total, g, parts):
-            for i, part in enumerate(parts):
+        def sum_and_turn(g, q, total):
+            for k in range(2 * M):
                 nc.tensor.matmul(
-                    out=total[:, g, :], lhsT=part, rhs=ident[:], is_transpose=True,
-                    start=(i == 0), stop=(i == len(parts) - 1),
+                    out=total[:, g, :], lhsT=terms[g][:, q, k, :], rhs=ident[:], is_transpose=True,
+                    start=(k == 0), stop=(k == 2 * M - 1),
                 )
 
-        def sum_pairs(g):
-            sum_and_turn(den_ps, g, [pairs[g][:, 0, j, :] for j in range(M)])
-            sum_and_turn(num_ps, g, [pairs[g][:, 1, j, :] for j in range(M)])
-
-        rsqrt = keep.tile([P, GROUPS, CH], F32)
+        squares = keep.tile([P, GROUPS, CH], F32)
         recip = keep.tile([P, GROUPS, CH], F32)
         result_rows = keep.tile([P, GROUPS, CH], F32)
 
-        def rsqrt_of_sum(g0, g1):
-            nc.scalar.activation(out=rsqrt[:, g0:g1, :], in_=den_ps[:, g0:g1, :], func=ACT.Abs_reciprocal_sqrt)
+        def square(out, in_):
+            nc.scalar.activation(out=out, in_=in_, func=ACT.Square)
 
-        def reciprocal_of_sum(g0, g1):
-            nc.scalar.activation(out=recip[:, g0:g1, :], in_=rsqrt[:, g0:g1, :], func=ACT.Square)
+        def rsqrt(out, in_):
+            nc.scalar.activation(out=out, in_=in_, func=ACT.Abs_reciprocal_sqrt)
 
         def finish(g0, g1):
             nc.vector.tensor_tensor(
@@ -268,9 +257,9 @@ def tile_tokencompressor_pa_kernel(tc, H, W_a_KV, W_b_KV, W_a_Z, W_b_Z, B_a, B_b
         quantise_w(ZA, ZA + 1)
         nc.vector.tensor_copy(out=bias[:], in_=bias_ps[:, 0 : 2 * M])
         transposes(1)
+        regroup_w(ZB)
         quantise_h(0)
         copies(1)
-        regroup_w(ZB)
         quantise_w(ZB, ZB + 1)
         quantise_h(1)
         transposes(2)
@@ -302,7 +291,7 @@ def tile_tokencompressor_pa_kernel(tc, H, W_a_KV, W_b_KV, W_a_Z, W_b_Z, B_a, B_b
         transposes(6)
         quantise_h(5)
         transposes(7)
-        copies(6, (1,))
+        copies(6)
         copies(7, (1,))
         project_z(2)
         project_z(3)
@@ -323,11 +312,12 @@ def tile_tokencompressor_pa_kernel(tc, H, W_a_KV, W_b_KV, W_a_Z, W_b_Z, B_a, B_b
             maximum_of_unit(u + 1)
             times_values(g - 1, 0)
             maximum_2(g)
-            times_values(g - 1, 1)
+            times_values(g - 1, 1, 0, 2)
             maximum_1(g)
-            if u + 2 < UNITS:
-                add_bias(u + 2)
-                add_bias(u + 3)
+            times_values(g - 1, 1, 2, 4)
+            times_edge_values(g - 1)
+            add_bias(u + 2)
+            add_bias(u + 3)
             project_c(u)
             project_c(u + 1)
             if u + 4 < UNITS:
@@ -339,31 +329,39 @@ def tile_tokencompressor_pa_kernel(tc, H, W_a_KV, W_b_KV, W_a_Z, W_b_Z, B_a, B_b
             exponentials(g, 1)
             if (g + 1) % GROUPS_PER_BATCH > 0:
                 copy_cb_edge(g)
-            sum_and_turn(den_ps, g - 1, [terms[g - 1][:, 0, k, :] for k in range(2 * M)])
-            sum_and_turn(num_ps, g - 1, [terms[g - 1][:, 1, k, :] for k in range(2 * M)])
+            sum_and_turn(g - 1, 0, den_ps)
+            sum_and_turn(g - 1, 1, num_ps)
 
         u = 2 * last
+        square(squares[:, 0 : last - 1, :], den_ps[:, 0 : last - 1, :])
         maximum_of_unit(u)
         maximum_of_unit(u + 1)
-        maximum_2(last)
-        maximum_1(last)
+        sum_and_turn(last - 1, 0, den_ps)
         project_c(u)
         project_c(u + 1)
-        sum_and_turn(den_ps, last - 1, [terms[last - 1][:, 0, k, :] for k in range(2 * M)])
-        subtract_max(last, 0)
-        exponentials(last, 0)
+        times_values(last - 1, 0, 0, 2)
+        maximum_2(last)
+        times_values(last - 1, 0, 2, 4)
+        maximum_1(last)
+        times_values(last - 1, 1, 0, 2)
+        subtract_max(last, 0, 0, 2)
+        exponentials(last, 0, 0, 2)
+        subtract_max(last, 0, 2, 4)
+        square(squares[:, last - 1, :], den_ps[:, last - 1, :])
+        exponentials(last, 0, 2, 4)
         subtract_max(last, 1)
         exponentials(last, 1)
-        times_values(last - 1, 0)
-        times_values(last - 1, 1)
+        times_values(last - 1, 1, 2, 4)
+        times_edge_values(last - 1)
+        sum_and_turn(last - 1, 1, num_ps)
+        sum_and_turn(last, 0, den_ps)
         times_values(last, 0)
         times_values(last, 1)
-        sum_and_turn(den_ps, last, [terms[last][:, 0, k, :] for k in range(2 * M)])
-        sum_and_turn(num_ps, last - 1, [terms[last - 1][:, 1, k, :] for k in range(2 * M)])
-        sum_and_turn(num_ps, last, [terms[last][:, 1, k, :] for k in range(2 * M)])
-        rsqrt_of_sum(0, last - 1)
-        rsqrt_of_sum(last - 1, GROUPS)
-        reciprocal_of_sum(0, last - 1)
-        reciprocal_of_sum(last - 1, GROUPS)
+        times_edge_values(last)
+        sum_and_turn(last, 1, num_ps)
+        rsqrt(recip[:, 0 : last - 1, :], squares[:, 0 : last - 1, :])
+        rsqrt(squares[:, last, :], den_ps[:, last, :])
+        rsqrt(recip[:, last - 1, :], squares[:, last - 1, :])
+        square(recip[:, last, :], squares[:, last, :])
         finish(0, last - 1)
         finish(last - 1, GROUPS)

@@ -148,10 +148,16 @@ def tile_tokencompressor_pa_kernel(tc, H, W_a_KV, W_b_KV, W_a_Z, W_b_Z, B_a, B_b
                     stop=(c == PASSES - 1),
                 )
 
-        def project_z(u):
+        def project_za(u):
             z_ps[u] = psum.tile([P, 2, HALF, GROUP], F32, name="z_ps", tag="bank", bufs=BANKS)
             project(u, ZA, z_ps[u][:, 0])
+
+        def project_zb(u):
             project(u, ZB, z_ps[u][:, 1])
+
+        def project_z(u):
+            project_za(u)
+            project_zb(u)
 
         def project_c(u):
             g, half = u // 2, u % 2
@@ -161,6 +167,12 @@ def tile_tokencompressor_pa_kernel(tc, H, W_a_KV, W_b_KV, W_a_Z, W_b_Z, B_a, B_b
             js = slice(HALF * half, HALF * (half + 1))
             project(u, CA, ca_ps[g][:, js, :])
             project(u, CB, cb_ps[g][:, js, :])
+
+        def project_values(g, w):
+            acc = psum.tile([P, M, GROUP], F32, name="c_ps", tag="bank", bufs=BANKS)
+            (ca_ps if w == CA else cb_ps)[g] = acc
+            for half in range(2):
+                project(2 * g + half, w, acc[:, HALF * half : HALF * (half + 1), :])
 
         def place(g):
             return g // GROUPS_PER_BATCH, GROUP * (g % GROUPS_PER_BATCH)
@@ -257,14 +269,15 @@ def tile_tokencompressor_pa_kernel(tc, H, W_a_KV, W_b_KV, W_a_Z, W_b_Z, B_a, B_b
         quantise_w(ZA, ZA + 1)
         nc.vector.tensor_copy(out=bias[:], in_=bias_ps[:, 0 : 2 * M])
         transposes(1)
-        regroup_w(ZB)
         quantise_h(0)
+        project_za(0)
+        regroup_w(ZB)
         copies(1)
         quantise_w(ZB, ZB + 1)
         quantise_h(1)
         transposes(2)
         copies(2)
-        project_z(0)
+        project_zb(0)
         regroup_w(CA)
         project_z(1)
         transposes(3)
@@ -320,6 +333,8 @@ def tile_tokencompressor_pa_kernel(tc, H, W_a_KV, W_b_KV, W_a_Z, W_b_Z, B_a, B_b
             add_bias(u + 3)
             project_c(u)
             project_c(u + 1)
+            if g == last - 1:
+                project_values(last, CA)
             if u + 4 < UNITS:
                 project_z(u + 4)
                 project_z(u + 5)
@@ -336,19 +351,15 @@ def tile_tokencompressor_pa_kernel(tc, H, W_a_KV, W_b_KV, W_a_Z, W_b_Z, B_a, B_b
         square(squares[:, 0 : last - 1, :], den_ps[:, 0 : last - 1, :])
         maximum_of_unit(u)
         maximum_of_unit(u + 1)
+        project_values(last, CB)
         sum_and_turn(last - 1, 0, den_ps)
-        project_c(u)
-        project_c(u + 1)
         times_values(last - 1, 0, 0, 2)
         maximum_2(last)
         times_values(last - 1, 0, 2, 4)
         maximum_1(last)
         times_values(last - 1, 1, 0, 2)
-        subtract_max(last, 0, 0, 2)
-        exponentials(last, 0, 0, 2)
-        subtract_max(last, 0, 2, 4)
-        square(squares[:, last - 1, :], den_ps[:, last - 1, :])
-        exponentials(last, 0, 2, 4)
+        subtract_max(last, 0)
+        exponentials(last, 0)
         subtract_max(last, 1)
         exponentials(last, 1)
         times_values(last - 1, 1, 2, 4)
@@ -359,9 +370,8 @@ def tile_tokencompressor_pa_kernel(tc, H, W_a_KV, W_b_KV, W_a_Z, W_b_Z, B_a, B_b
         times_values(last, 1)
         times_edge_values(last)
         sum_and_turn(last, 1, num_ps)
+        rsqrt(squares[:, last - 1 : GROUPS, :], den_ps[:, last - 1 : GROUPS, :])
         rsqrt(recip[:, 0 : last - 1, :], squares[:, 0 : last - 1, :])
-        rsqrt(squares[:, last, :], den_ps[:, last, :])
-        rsqrt(recip[:, last - 1, :], squares[:, last - 1, :])
-        square(recip[:, last, :], squares[:, last, :])
+        square(recip[:, last - 1 : GROUPS, :], squares[:, last - 1 : GROUPS, :])
         finish(0, last - 1)
         finish(last - 1, GROUPS)

@@ -238,6 +238,21 @@ def tile_tokencompressor_pa_kernel(tc, H, W_a_KV, W_b_KV, W_a_Z, W_b_Z, B_a, B_b
                 out=terms[g][:, 1, ks, 0:1], in0=terms[g][:, 0, ks, 0:1], in1=cb_edge[:, g], op=ALU.mult
             )
 
+        pairs = {}
+
+        def add_pairs(g, q):
+            pairs[g, q] = work.tile([P, M, GROUP], F32, name="pairs", tag="pairs", bufs=4)
+            nc.vector.tensor_tensor(
+                out=pairs[g, q][:], in0=terms[g][:, q, 0:M, :], in1=terms[g][:, q, M : 2 * M, :], op=ALU.add
+            )
+
+        def sum_pairs(g, q, total):
+            for j in range(M):
+                nc.tensor.matmul(
+                    out=total[:, g, :], lhsT=pairs[g, q][:, j, :], rhs=ident[:], is_transpose=True,
+                    start=(j == 0), stop=(j == M - 1),
+                )
+
         def sum_and_turn(g, q, total):
             for k in range(2 * M):
                 nc.tensor.matmul(
@@ -261,6 +276,7 @@ def tile_tokencompressor_pa_kernel(tc, H, W_a_KV, W_b_KV, W_a_Z, W_b_Z, B_a, B_b
             )
             nc.sync.dma_start(out=out_rows[:, g0:g1, :], in_=result_rows[:, g0:g1, :])
 
+        last = GROUPS - 1
         transposes(0)
         nc.vector.tensor_copy(out=bias_rows32[:], in_=bias_rows[:])
         nc.tensor.transpose(out=bias_ps[:], in_=bias_rows32[:], identity=ident[:])
@@ -289,87 +305,96 @@ def tile_tokencompressor_pa_kernel(tc, H, W_a_KV, W_b_KV, W_a_Z, W_b_Z, B_a, B_b
         quantise_w(CA, CB + 1)
         maximum_of_unit(1)
         copies(3)
+        project_z(2)
         transposes(4)
         maximum_2(0)
         quantise_h(3)
         maximum_1(0)
+        add_bias(2)
         copies(4)
+        project_z(3)
+        project_values(0, CA)
         transposes(5)
         subtract_max(0, 0)
         subtract_max(0, 1)
-        quantise_h(4)
-        copies(5)
+        maximum_of_unit(2)
+        add_bias(3)
         exponentials(0, 0)
         exponentials(0, 1)
+        quantise_h(4)
+        maximum_of_unit(3)
+        copies(5)
+        project_values(0, CB)
         transposes(6)
+        times_values(0, 0)
+        maximum_2(1)
+        add_pairs(0, 0)
         quantise_h(5)
-        transposes(7)
-        copies(6)
-        copies(7, (1,))
-        project_z(2)
-        project_z(3)
-        quantise_h(6)
-        project_c(0)
-        project_c(1)
-        quantise_h(7)
-        add_bias(2)
-        add_bias(3)
-        project_z(4)
-        project_z(5)
+        maximum_1(1)
         copy_cb_edge(0)
-
-        last = GROUPS - 1
-        for g in range(1, last):
-            u = 2 * g
-            maximum_of_unit(u)
-            maximum_of_unit(u + 1)
-            times_values(g - 1, 0)
-            maximum_2(g)
-            times_values(g - 1, 1, 0, 2)
-            maximum_1(g)
-            times_values(g - 1, 1, 2, 4)
-            times_edge_values(g - 1)
-            add_bias(u + 2)
-            add_bias(u + 3)
-            project_c(u)
-            project_c(u + 1)
-            if g == last - 1:
-                project_values(last, CA)
-            if u + 4 < UNITS:
-                project_z(u + 4)
-                project_z(u + 5)
-            subtract_max(g, 0)
-            exponentials(g, 0)
-            subtract_max(g, 1)
-            exponentials(g, 1)
-            if (g + 1) % GROUPS_PER_BATCH > 0:
-                copy_cb_edge(g)
-            sum_and_turn(g - 1, 0, den_ps)
-            sum_and_turn(g - 1, 1, num_ps)
-
-        u = 2 * last
+        copies(6)
+        times_values(0, 1)
+        times_edge_values(0)
+        project_z(4)
+        transposes(7)
+        subtract_max(1, 0)
+        subtract_max(1, 1)
+        add_bias(4)
+        quantise_h(6)
+        copies(7)
+        maximum_of_unit(4)
+        project_z(5)
+        add_bias(5)
+        exponentials(1, 0)
+        exponentials(1, 1)
+        quantise_h(7)
+        project_c(2)
+        project_c(3)
+        project_z(6)
+        project_z(7)
+        sum_pairs(0, 0, den_ps)
+        sum_and_turn(0, 1, num_ps)
+        add_bias(6)
+        add_bias(7)
+        maximum_of_unit(5)
+        times_values(1, 0)
+        maximum_2(2)
+        times_values(1, 1, 0, 2)
+        maximum_1(2)
+        times_values(1, 1, 2, 4)
+        times_edge_values(1)
+        subtract_max(2, 0)
+        exponentials(2, 0)
+        subtract_max(2, 1)
+        exponentials(2, 1)
+        project_c(4)
+        project_c(5)
+        project_values(3, CA)
+        copy_cb_edge(2)
+        sum_and_turn(1, 0, den_ps)
+        sum_and_turn(1, 1, num_ps)
         square(squares[:, 0 : last - 1, :], den_ps[:, 0 : last - 1, :])
-        maximum_of_unit(u)
-        maximum_of_unit(u + 1)
-        project_values(last, CB)
-        sum_and_turn(last - 1, 0, den_ps)
-        times_values(last - 1, 0, 0, 2)
-        maximum_2(last)
-        times_values(last - 1, 0, 2, 4)
-        maximum_1(last)
-        times_values(last - 1, 1, 0, 2)
-        subtract_max(last, 0)
-        exponentials(last, 0)
-        subtract_max(last, 1)
-        exponentials(last, 1)
-        times_values(last - 1, 1, 2, 4)
-        times_edge_values(last - 1)
-        sum_and_turn(last - 1, 1, num_ps)
-        sum_and_turn(last, 0, den_ps)
-        times_values(last, 0)
-        times_values(last, 1)
-        times_edge_values(last)
-        sum_and_turn(last, 1, num_ps)
+        maximum_of_unit(6)
+        maximum_of_unit(7)
+        project_values(3, CB)
+        sum_and_turn(2, 0, den_ps)
+        times_values(2, 0, 0, 2)
+        maximum_2(3)
+        times_values(2, 0, 2, 4)
+        maximum_1(3)
+        times_values(2, 1, 0, 2)
+        subtract_max(3, 0)
+        exponentials(3, 0)
+        subtract_max(3, 1)
+        exponentials(3, 1)
+        times_values(2, 1, 2, 4)
+        times_edge_values(2)
+        sum_and_turn(2, 1, num_ps)
+        sum_and_turn(3, 0, den_ps)
+        times_values(3, 0)
+        times_values(3, 1)
+        times_edge_values(3)
+        sum_and_turn(3, 1, num_ps)
         rsqrt(squares[:, last - 1 : GROUPS, :], den_ps[:, last - 1 : GROUPS, :])
         rsqrt(recip[:, 0 : last - 1, :], squares[:, 0 : last - 1, :])
         square(recip[:, last - 1 : GROUPS, :], squares[:, last - 1 : GROUPS, :])

@@ -105,7 +105,7 @@ def tile_tokencompressor_pa_kernel(tc, H, W_a_KV, W_b_KV, W_a_Z, W_b_Z, B_a, B_b
 
         xt, h_grouped, h_codes, h_scales = {}, {}, {}, {}
         z_ps, cb_ps, ca_ps = {}, {}, {}
-        max4, max2, max1, terms = {}, {}, {}, {}
+        max4, max1, terms = {}, {}, {}
 
         def transposes(u):
             h_words = h_raw[u // 2].bitcast(F32)
@@ -203,13 +203,11 @@ def tile_tokencompressor_pa_kernel(tc, H, W_a_KV, W_b_KV, W_a_Z, W_b_Z, B_a, B_b
                 out=max4[g][:, js, :], in0=logits(g)[:, 0:M, :][:, js, :], in1=logits(g)[:, M : 2 * M, :][:, js, :], op=ALU.max
             )
 
-        def maximum_2(g):
-            max2[g] = work.tile([P, 2, GROUP], F32, name="max2", tag="max2")
-            nc.vector.tensor_tensor(out=max2[g][:], in0=max4[g][:, 0:2, :], in1=max4[g][:, 2:4, :], op=ALU.max)
-
-        def maximum_1(g):
+        def maximum_of_positions(g):
             max1[g] = work.tile([P, 1, GROUP], F32, name="max1", tag="max1")
-            nc.vector.tensor_tensor(out=max1[g][:], in0=max2[g][:, 0:1, :], in1=max2[g][:, 1:2, :], op=ALU.max)
+            nc.vector.tensor_reduce(
+                out=max1[g][:, 0, :], in_=max4[g].rearrange("p k i -> p i k"), op=ALU.max, axis=mybir.AxisListType.X
+            )
 
         def subtract_max(g, s, j0=0, j1=M):
             if s == 0 and j0 == 0:
@@ -298,8 +296,8 @@ def tile_tokencompressor_pa_kernel(tc, H, W_a_KV, W_b_KV, W_a_Z, W_b_Z, B_a, B_b
         project_z(1)
         transposes(3)
         add_bias(0)
-        quantise_h(2)
         regroup_w(CB)
+        quantise_h(2)
         maximum_of_unit(0)
         add_bias(1)
         quantise_w(CA, CB + 1)
@@ -307,14 +305,13 @@ def tile_tokencompressor_pa_kernel(tc, H, W_a_KV, W_b_KV, W_a_Z, W_b_Z, B_a, B_b
         copies(3)
         project_z(2)
         transposes(4)
-        maximum_2(0)
+        maximum_of_positions(0)
         quantise_h(3)
-        maximum_1(0)
         add_bias(2)
         copies(4)
         project_z(3)
-        project_values(0, CA)
         transposes(5)
+        project_values(0, CA)
         subtract_max(0, 0)
         subtract_max(0, 1)
         maximum_of_unit(2)
@@ -327,14 +324,13 @@ def tile_tokencompressor_pa_kernel(tc, H, W_a_KV, W_b_KV, W_a_Z, W_b_Z, B_a, B_b
         project_values(0, CB)
         transposes(6)
         times_values(0, 0)
-        maximum_2(1)
+        maximum_of_positions(1)
         add_pairs(0, 0)
-        quantise_h(5)
-        maximum_1(1)
         copy_cb_edge(0)
         copies(6)
         times_values(0, 1)
         times_edge_values(0)
+        quantise_h(5)
         project_z(4)
         transposes(7)
         subtract_max(1, 0)
@@ -358,10 +354,8 @@ def tile_tokencompressor_pa_kernel(tc, H, W_a_KV, W_b_KV, W_a_Z, W_b_Z, B_a, B_b
         add_bias(7)
         maximum_of_unit(5)
         times_values(1, 0)
-        maximum_2(2)
-        times_values(1, 1, 0, 2)
-        maximum_1(2)
-        times_values(1, 1, 2, 4)
+        maximum_of_positions(2)
+        times_values(1, 1)
         times_edge_values(1)
         subtract_max(2, 0)
         exponentials(2, 0)
@@ -379,15 +373,13 @@ def tile_tokencompressor_pa_kernel(tc, H, W_a_KV, W_b_KV, W_a_Z, W_b_Z, B_a, B_b
         project_values(3, CB)
         sum_and_turn(2, 0, den_ps)
         times_values(2, 0, 0, 2)
-        maximum_2(3)
+        maximum_of_positions(3)
         times_values(2, 0, 2, 4)
-        maximum_1(3)
-        times_values(2, 1, 0, 2)
         subtract_max(3, 0)
         exponentials(3, 0)
         subtract_max(3, 1)
         exponentials(3, 1)
-        times_values(2, 1, 2, 4)
+        times_values(2, 1)
         times_edge_values(2)
         sum_and_turn(2, 1, num_ps)
         sum_and_turn(3, 0, den_ps)

@@ -105,7 +105,7 @@ def tile_tokencompressor_pa_kernel(tc, H, W_a_KV, W_b_KV, W_a_Z, W_b_Z, B_a, B_b
 
         xt, h_grouped, h_codes, h_scales = {}, {}, {}, {}
         z_ps, cb_ps, ca_ps = {}, {}, {}
-        max4, max1, terms = {}, {}, {}
+        max4, max2, max1, terms = {}, {}, {}, {}
 
         def transposes(u):
             h_words = h_raw[u // 2].bitcast(F32)
@@ -203,11 +203,13 @@ def tile_tokencompressor_pa_kernel(tc, H, W_a_KV, W_b_KV, W_a_Z, W_b_Z, B_a, B_b
                 out=max4[g][:, js, :], in0=logits(g)[:, 0:M, :][:, js, :], in1=logits(g)[:, M : 2 * M, :][:, js, :], op=ALU.max
             )
 
-        def maximum_of_positions(g):
+        def maximum_2(g):
+            max2[g] = work.tile([P, 2, GROUP], F32, name="max2", tag="max2")
+            nc.vector.tensor_tensor(out=max2[g][:], in0=max4[g][:, 0:2, :], in1=max4[g][:, 2:4, :], op=ALU.max)
+
+        def maximum_1(g):
             max1[g] = work.tile([P, 1, GROUP], F32, name="max1", tag="max1")
-            nc.vector.tensor_reduce(
-                out=max1[g][:, 0, :], in_=max4[g].rearrange("p k i -> p i k"), op=ALU.max, axis=mybir.AxisListType.X
-            )
+            nc.vector.tensor_tensor(out=max1[g][:], in0=max2[g][:, 0:1, :], in1=max2[g][:, 1:2, :], op=ALU.max)
 
         def subtract_max(g, s, j0=0, j1=M):
             if s == 0 and j0 == 0:
@@ -268,11 +270,11 @@ def tile_tokencompressor_pa_kernel(tc, H, W_a_KV, W_b_KV, W_a_Z, W_b_Z, B_a, B_b
         def rsqrt(out, in_):
             nc.scalar.activation(out=out, in_=in_, func=ACT.Abs_reciprocal_sqrt)
 
-        def finish(g0, g1):
+        def finish(g0, g1, queue):
             nc.vector.tensor_tensor(
                 out=result_rows[:, g0:g1, :], in0=num_ps[:, g0:g1, :], in1=recip[:, g0:g1, :], op=ALU.mult
             )
-            nc.sync.dma_start(out=out_rows[:, g0:g1, :], in_=result_rows[:, g0:g1, :])
+            queue.dma_start(out=out_rows[:, g0:g1, :], in_=result_rows[:, g0:g1, :])
 
         last = GROUPS - 1
         transposes(0)
@@ -305,8 +307,9 @@ def tile_tokencompressor_pa_kernel(tc, H, W_a_KV, W_b_KV, W_a_Z, W_b_Z, B_a, B_b
         copies(3)
         project_z(2)
         transposes(4)
-        maximum_of_positions(0)
+        maximum_2(0)
         quantise_h(3)
+        maximum_1(0)
         add_bias(2)
         copies(4)
         project_z(3)
@@ -324,8 +327,9 @@ def tile_tokencompressor_pa_kernel(tc, H, W_a_KV, W_b_KV, W_a_Z, W_b_Z, B_a, B_b
         project_values(0, CB)
         transposes(6)
         times_values(0, 0)
-        maximum_of_positions(1)
+        maximum_2(1)
         add_pairs(0, 0)
+        maximum_1(1)
         copy_cb_edge(0)
         copies(6)
         times_values(0, 1)
@@ -354,8 +358,10 @@ def tile_tokencompressor_pa_kernel(tc, H, W_a_KV, W_b_KV, W_a_Z, W_b_Z, B_a, B_b
         add_bias(7)
         maximum_of_unit(5)
         times_values(1, 0)
-        maximum_of_positions(2)
-        times_values(1, 1)
+        maximum_2(2)
+        times_values(1, 1, 0, 2)
+        maximum_1(2)
+        times_values(1, 1, 2, 4)
         times_edge_values(1)
         subtract_max(2, 0)
         exponentials(2, 0)
@@ -373,13 +379,19 @@ def tile_tokencompressor_pa_kernel(tc, H, W_a_KV, W_b_KV, W_a_Z, W_b_Z, B_a, B_b
         project_values(3, CB)
         sum_and_turn(2, 0, den_ps)
         times_values(2, 0, 0, 2)
-        maximum_of_positions(3)
+        maximum_2(3)
         times_values(2, 0, 2, 4)
-        subtract_max(3, 0)
-        exponentials(3, 0)
-        subtract_max(3, 1)
-        exponentials(3, 1)
-        times_values(2, 1)
+        maximum_1(3)
+        times_values(2, 1, 0, 2)
+        subtract_max(3, 0, 0, 2)
+        exponentials(3, 0, 0, 2)
+        subtract_max(3, 0, 2, 4)
+        exponentials(3, 0, 2, 4)
+        subtract_max(3, 1, 0, 2)
+        exponentials(3, 1, 0, 2)
+        subtract_max(3, 1, 2, 4)
+        exponentials(3, 1, 2, 4)
+        times_values(2, 1, 2, 4)
         times_edge_values(2)
         sum_and_turn(2, 1, num_ps)
         sum_and_turn(3, 0, den_ps)
@@ -390,5 +402,5 @@ def tile_tokencompressor_pa_kernel(tc, H, W_a_KV, W_b_KV, W_a_Z, W_b_Z, B_a, B_b
         rsqrt(squares[:, last - 1 : GROUPS, :], den_ps[:, last - 1 : GROUPS, :])
         rsqrt(recip[:, 0 : last - 1, :], squares[:, 0 : last - 1, :])
         square(recip[:, last - 1 : GROUPS, :], squares[:, last - 1 : GROUPS, :])
-        finish(0, last - 1)
-        finish(last - 1, GROUPS)
+        finish(0, last - 1, nc.sync)
+        finish(last - 1, GROUPS, nc.scalar)

from contextlib import ExitStack

import concourse.mybir as mybir
from concourse.masks import make_identity

F32 = mybir.dt.float32
BF16 = mybir.dt.bfloat16
U32 = mybir.dt.uint32
U8 = mybir.dt.uint8
FP8X4 = mybir.dt.float8_e4m3fn_x4
ACT = mybir.ActivationFunctionType
ALU = mybir.AluOpType

P = 128
BATCH = 2
TOKENS = 1024
D = 1024
CH = 128
M = 4
K_PASS = 512
PASSES = D // K_PASS
GROUP = 128
GROUPS = BATCH * TOKENS // (M * GROUP)
GROUPS_PER_BATCH = GROUPS // BATCH
BLOCKS = TOKENS // M
HALF = M // 2
UNITS = 2 * GROUPS
UNIT_COLS = HALF * GROUP
NEG = -1e30
ZA, ZB, CA, CB = 0, 1, 2, 3

BANKS = 6

FLOPS = 2 * BATCH * TOKENS * D * 4 * CH


def tile_tokencompressor_pa_kernel(tc, H, W_a_KV, W_b_KV, W_a_Z, W_b_Z, B_a, B_b, out):
    nc = tc.nc
    weights = [W_a_Z, W_b_Z, W_a_KV, W_b_KV]
    h_groups = H.flatten_outer_dims().rearrange("(g i j) d -> g i j d", i=GROUP, j=M)
    out_rows = out.flatten_outer_dims().rearrange("(g i) c -> i g c", i=GROUP)

    with ExitStack() as stack:
        keep = stack.enter_context(tc.tile_pool(name="keep", bufs=1))
        work = stack.enter_context(tc.tile_pool(name="work", bufs=2))
        psum = stack.enter_context(tc.psum_pool(name="psum", bufs=1))
        stack.enter_context(tc.manual_schedule())

        h_raw = [keep.tile([P, M, D], BF16, name="h_raw%d" % g) for g in range(GROUPS)]
        w_raw = keep.tile([P, 4, PASSES, 4, CH], BF16)
        bias_rows = keep.tile([P, P], BF16)

        def load_h(u):
            js = slice(HALF * (u % 2), HALF * (u % 2 + 1))
            nc.sync.dma_start(out=h_raw[u // 2][:, js, :], in_=h_groups[u // 2][:, js, :])

        def load_w(w):
            nc.sync.dma_start(
                out=w_raw[:, w],
                in_=weights[w].rearrange("(c p t) n -> p c t n", c=PASSES, t=4),
            )

        nc.vector.memset(bias_rows[:], 0.0)
        load_h(0)
        nc.sync.dma_start(out=bias_rows[0:M, :], in_=B_a)
        nc.sync.dma_start(out=bias_rows[M : 2 * M, :], in_=B_b)
        load_w(ZA)
        load_h(1)
        load_w(ZB)
        load_h(2)
        load_w(CA)
        load_w(CB)
        for u in range(3, UNITS):
            load_h(u)

        ident = keep.tile([P, P], F32)
        make_identity(nc, ident[:])

        z_all = [keep.tile([P, 2 * M, BLOCKS + 1], F32, name="z_all%d" % n) for n in range(BATCH)]
        for n in range(BATCH):
            nc.vector.memset(z_all[n][:, M : 2 * M, 0:1], NEG)
        cb_edge = keep.tile([P, GROUPS, M, 1], F32)
        nc.vector.memset(cb_edge[:], 0.0)
        den_ps = psum.tile([P, GROUPS, CH], F32)
        num_ps = psum.tile([P, GROUPS, CH], F32)

        bias_rows32 = keep.tile([P, P], F32)
        bias = keep.tile([P, 2 * M], F32)

        bias_ps = psum.tile([P, P], F32, tag="bank", bufs=BANKS)

        w_grouped = keep.tile([P, 4, PASSES, CH, 4], BF16, align_bytes=64)
        w_codes = keep.tile([P, 4, PASSES, CH], U32, align_bytes=64)
        w_scales = keep.tile([P, 4, PASSES, CH], U8, align_bytes=64)

        def regroup_w(w):
            nc.vector.tensor_copy(out=w_grouped[:, w], in_=w_raw[:, w].rearrange("p c t n -> p c n t"))

        def quantise_w(w0, w1):
            nc.vector.quantize_mx(
                out=w_codes[:, w0:w1].rearrange("p w c n -> p (w c n)").bitcast(FP8X4),
                scales=w_scales[:, w0:w1].rearrange("p w c n -> p (w c n)"),
                in_=w_grouped[:, w0:w1].rearrange("p w c n t -> p (w c n t)"),
            )

        xt, h_grouped, h_codes, h_scales = {}, {}, {}, {}
        z_ps, cb_ps, ca_ps = {}, {}, {}
        max4, max2, max1, terms = {}, {}, {}, {}

        def transposes(u):
            h_words = h_raw[u // 2].bitcast(F32)
            for c in range(PASSES):
                xt[u, c] = psum.tile([P, 2, HALF, GROUP], F32, name="xt", tag="bank", bufs=BANKS)
                for v in range(2):
                    for jj in range(HALF):
                        first = 256 * c + v
                        nc.tensor.transpose(
                            out=xt[u, c][:, v, jj, :],
                            in_=h_words[:, HALF * (u % 2) + jj, first : 256 * (c + 1) : 2],
                            identity=ident[:],
                        )

        def copies(u, vector_passes=()):
            h_grouped[u] = work.tile([P, PASSES, UNIT_COLS, 4], BF16, align_bytes=64, name="h_grouped", tag="h_grouped", bufs=4)
            h_grouped_words = h_grouped[u].bitcast(F32)
            for c in range(PASSES):
                copy = nc.vector.tensor_copy if c in vector_passes else nc.scalar.copy
                copy(out=h_grouped_words[:, c, :, :], in_=xt[u, c].rearrange("p v jj i -> p (jj i) v"))

        def quantise_h(u):
            h_codes[u] = work.tile([P, PASSES, UNIT_COLS], U32, align_bytes=64, name="h_codes", tag="h_codes", bufs=UNITS)
            h_scales[u] = work.tile([P, PASSES, UNIT_COLS], U8, align_bytes=64, name="h_scales", tag="h_scales", bufs=UNITS)
            nc.vector.quantize_mx(
                out=h_codes[u].rearrange("p c col -> p (c col)").bitcast(FP8X4),
                scales=h_scales[u].rearrange("p c col -> p (c col)"),
                in_=h_grouped[u].rearrange("p c col t -> p (c col t)"),
            )

        def project(u, w, acc):
            for c in range(PASSES):
                nc.tensor.matmul_mx(
                    out=acc.rearrange("p jj i -> p (jj i)"),
                    lhsT=w_codes[:, w, c, :].bitcast(FP8X4),
                    lhsT_scale=w_scales[:, w, c, :],
                    rhs=h_codes[u][:, c, :].bitcast(FP8X4),
                    rhs_scale=h_scales[u][:, c, :],
                    start=(c == 0),
                    stop=(c == PASSES - 1),
                )

        def project_za(u):
            z_ps[u] = psum.tile([P, 2, HALF, GROUP], F32, name="z_ps", tag="bank", bufs=BANKS)
            project(u, ZA, z_ps[u][:, 0])

        def project_zb(u):
            project(u, ZB, z_ps[u][:, 1])

        def project_z(u):
            project_za(u)
            project_zb(u)

        def project_c(u):
            g, half = u // 2, u % 2
            if half == 0:
                ca_ps[g] = psum.tile([P, M, GROUP], F32, name="ca_ps", tag="bank", bufs=BANKS)
                cb_ps[g] = psum.tile([P, M, GROUP], F32, name="cb_ps", tag="bank", bufs=BANKS)
            js = slice(HALF * half, HALF * (half + 1))
            project(u, CA, ca_ps[g][:, js, :])
            project(u, CB, cb_ps[g][:, js, :])

        def project_values(g, w):
            acc = psum.tile([P, M, GROUP], F32, name="c_ps", tag="bank", bufs=BANKS)
            (ca_ps if w == CA else cb_ps)[g] = acc
            for half in range(2):
                project(2 * g + half, w, acc[:, HALF * half : HALF * (half + 1), :])

        def place(g):
            return g // GROUPS_PER_BATCH, GROUP * (g % GROUPS_PER_BATCH)

        def add_bias(u):
            n, first = place(u // 2)
            for s in range(2):
                for jj in range(HALF):
                    k = M * s + HALF * (u % 2) + jj
                    nc.scalar.activation(
                        out=z_all[n][:, k, first + s : first + s + GROUP], in_=z_ps[u][:, s, jj, :],
                        func=ACT.Identity, bias=bias[:, k : k + 1], scale=1.0,
                    )

        def copy_cb_edge(g):
            nc.scalar.copy(out=cb_edge[:, g + 1], in_=cb_ps[g][:, :, GROUP - 1 : GROUP])

        def logits(g):
            n, first = place(g)
            return z_all[n][:, :, first : first + GROUP]

        def maximum_of_unit(u):
            g, half = u // 2, u % 2
            if half == 0:
                max4[g] = work.tile([P, M, GROUP], F32, name="max4", tag="max4")
            js = slice(HALF * half, HALF * (half + 1))
            nc.vector.tensor_tensor(
                out=max4[g][:, js, :], in0=logits(g)[:, 0:M, :][:, js, :], in1=logits(g)[:, M : 2 * M, :][:, js, :], op=ALU.max
            )

        def maximum_2(g):
            max2[g] = work.tile([P, 2, GROUP], F32, name="max2", tag="max2")
            nc.vector.tensor_tensor(out=max2[g][:], in0=max4[g][:, 0:2, :], in1=max4[g][:, 2:4, :], op=ALU.max)

        def maximum_1(g):
            max1[g] = work.tile([P, 1, GROUP], F32, name="max1", tag="max1")
            nc.vector.tensor_tensor(out=max1[g][:], in0=max2[g][:, 0:1, :], in1=max2[g][:, 1:2, :], op=ALU.max)

        def subtract_max(g, s, j0=0, j1=M):
            if s == 0 and j0 == 0:
                terms[g] = work.tile([P, 2, 2 * M, GROUP], F32, name="terms", tag="terms", bufs=3)
            ks = slice(M * s + j0, M * s + j1)
            nc.vector.tensor_tensor(
                out=terms[g][:, 0, ks, :], in0=logits(g)[:, ks, :],
                in1=max1[g].to_broadcast([P, j1 - j0, GROUP]), op=ALU.subtract,
            )

        def exponentials(g, s, j0=0, j1=M):
            ks = slice(M * s + j0, M * s + j1)
            nc.scalar.activation(out=terms[g][:, 0, ks, :], in_=terms[g][:, 0, ks, :], func=ACT.Exp)

        def times_values(g, s, j0=0, j1=M):
            ks = slice(M * s + j0, M * s + j1)
            shift = s
            nc.vector.tensor_tensor(
                out=terms[g][:, 1, ks, shift:], in0=terms[g][:, 0, ks, shift:],
                in1=(ca_ps, cb_ps)[s][g][:, j0:j1, 0 : GROUP - shift], op=ALU.mult,
            )

        def times_edge_values(g):
            ks = slice(M, 2 * M)
            nc.vector.tensor_tensor(
                out=terms[g][:, 1, ks, 0:1], in0=terms[g][:, 0, ks, 0:1], in1=cb_edge[:, g], op=ALU.mult
            )

        pairs = {}

        def add_pairs(g, q):
            pairs[g, q] = work.tile([P, M, GROUP], F32, name="pairs", tag="pairs", bufs=4)
            nc.vector.tensor_tensor(
                out=pairs[g, q][:], in0=terms[g][:, q, 0:M, :], in1=terms[g][:, q, M : 2 * M, :], op=ALU.add
            )

        def sum_pairs(g, q, total):
            for j in range(M):
                nc.tensor.matmul(
                    out=total[:, g, :], lhsT=pairs[g, q][:, j, :], rhs=ident[:], is_transpose=True,
                    start=(j == 0), stop=(j == M - 1),
                )

        def sum_and_turn(g, q, total):
            for k in range(2 * M):
                nc.tensor.matmul(
                    out=total[:, g, :], lhsT=terms[g][:, q, k, :], rhs=ident[:], is_transpose=True,
                    start=(k == 0), stop=(k == 2 * M - 1),
                )

        squares = keep.tile([P, GROUPS, CH], F32)
        recip = keep.tile([P, GROUPS, CH], F32)
        result_rows = keep.tile([P, GROUPS, CH], F32)

        def square(out, in_):
            nc.scalar.activation(out=out, in_=in_, func=ACT.Square)

        def rsqrt(out, in_):
            nc.scalar.activation(out=out, in_=in_, func=ACT.Abs_reciprocal_sqrt)

        def finish(g0, g1, queue):
            nc.vector.tensor_tensor(
                out=result_rows[:, g0:g1, :], in0=num_ps[:, g0:g1, :], in1=recip[:, g0:g1, :], op=ALU.mult
            )
            queue.dma_start(out=out_rows[:, g0:g1, :], in_=result_rows[:, g0:g1, :])

        last = GROUPS - 1
        transposes(0)
        nc.vector.tensor_copy(out=bias_rows32[:], in_=bias_rows[:])
        nc.tensor.transpose(out=bias_ps[:], in_=bias_rows32[:], identity=ident[:])
        copies(0)
        regroup_w(ZA)
        quantise_w(ZA, ZA + 1)
        nc.vector.tensor_copy(out=bias[:], in_=bias_ps[:, 0 : 2 * M])
        transposes(1)
        quantise_h(0)
        project_za(0)
        regroup_w(ZB)
        copies(1)
        quantise_w(ZB, ZB + 1)
        quantise_h(1)
        transposes(2)
        copies(2)
        project_zb(0)
        regroup_w(CA)
        project_z(1)
        transposes(3)
        add_bias(0)
        regroup_w(CB)
        quantise_h(2)
        maximum_of_unit(0)
        add_bias(1)
        quantise_w(CA, CB + 1)
        maximum_of_unit(1)
        copies(3)
        project_z(2)
        transposes(4)
        maximum_2(0)
        quantise_h(3)
        maximum_1(0)
        add_bias(2)
        copies(4)
        project_z(3)
        transposes(5)
        project_values(0, CA)
        subtract_max(0, 0)
        subtract_max(0, 1)
        maximum_of_unit(2)
        add_bias(3)
        exponentials(0, 0)
        exponentials(0, 1)
        quantise_h(4)
        maximum_of_unit(3)
        copies(5)
        project_values(0, CB)
        transposes(6)
        times_values(0, 0)
        maximum_2(1)
        add_pairs(0, 0)
        maximum_1(1)
        copy_cb_edge(0)
        copies(6)
        times_values(0, 1)
        times_edge_values(0)
        quantise_h(5)
        project_z(4)
        transposes(7)
        subtract_max(1, 0)
        subtract_max(1, 1)
        add_bias(4)
        quantise_h(6)
        copies(7)
        maximum_of_unit(4)
        project_z(5)
        add_bias(5)
        exponentials(1, 0)
        exponentials(1, 1)
        quantise_h(7)
        project_c(2)
        project_c(3)
        project_z(6)
        project_z(7)
        sum_pairs(0, 0, den_ps)
        sum_and_turn(0, 1, num_ps)
        add_bias(6)
        add_bias(7)
        maximum_of_unit(5)
        times_values(1, 0)
        maximum_2(2)
        times_values(1, 1, 0, 2)
        maximum_1(2)
        times_values(1, 1, 2, 4)
        times_edge_values(1)
        subtract_max(2, 0)
        exponentials(2, 0)
        subtract_max(2, 1)
        exponentials(2, 1)
        project_c(4)
        project_c(5)
        project_values(3, CA)
        copy_cb_edge(2)
        sum_and_turn(1, 0, den_ps)
        sum_and_turn(1, 1, num_ps)
        square(squares[:, 0 : last - 1, :], den_ps[:, 0 : last - 1, :])
        maximum_of_unit(6)
        maximum_of_unit(7)
        project_values(3, CB)
        sum_and_turn(2, 0, den_ps)
        times_values(2, 0, 0, 2)
        maximum_2(3)
        times_values(2, 0, 2, 4)
        maximum_1(3)
        times_values(2, 1, 0, 2)
        subtract_max(3, 0, 0, 2)
        exponentials(3, 0, 0, 2)
        subtract_max(3, 0, 2, 4)
        exponentials(3, 0, 2, 4)
        subtract_max(3, 1, 0, 2)
        exponentials(3, 1, 0, 2)
        subtract_max(3, 1, 2, 4)
        exponentials(3, 1, 2, 4)
        times_values(2, 1, 2, 4)
        times_edge_values(2)
        sum_and_turn(2, 1, num_ps)
        sum_and_turn(3, 0, den_ps)
        times_values(3, 0)
        times_values(3, 1)
        times_edge_values(3)
        sum_and_turn(3, 1, num_ps)
        rsqrt(squares[:, last - 1 : GROUPS, :], den_ps[:, last - 1 : GROUPS, :])
        rsqrt(recip[:, 0 : last - 1, :], squares[:, 0 : last - 1, :])
        square(recip[:, last - 1 : GROUPS, :], squares[:, last - 1 : GROUPS, :])
        finish(0, last - 1, nc.sync)
        finish(last - 1, GROUPS, nc.scalar)
